import numpy as np
import ml_dtypes


def mxq(x, axis, fmt="e4m3"):
    dtype, down = {"e4m3": (ml_dtypes.float8_e4m3fn, 7), "e5m2": (ml_dtypes.float8_e5m2, 14)}[fmt]
    v = np.moveaxis(np.asarray(x, np.float32).astype(ml_dtypes.bfloat16).astype(np.float64), axis, -1)
    blocks = v.reshape(v.shape[:-1] + (-1, 32))
    amax = np.abs(blocks).max(-1, keepdims=True)
    byte = np.maximum(np.where(amax > 0, np.frexp(amax)[1] - 1 + 127, 0) - down, 1)
    scale = np.exp2(byte - 127.0)
    codes = (blocks / scale).astype(np.float32).astype(dtype).astype(np.float64)
    return np.moveaxis((codes * scale).reshape(v.shape), -1, axis)


WIDE = False


def mx_kscale(k):
    if not WIDE:
        return np.ones(k)
    levels = np.array([10, -10, 5, -5, 0])
    if k % 512:
        return np.exp2(np.random.permutation(np.resize(levels, k // 32))).repeat(32)
    a = np.empty((k // 512, 16))
    for p in range(k // 512):
        a[p, :8] = np.random.permutation(np.resize(levels, 8))
        for g in range(8):
            far = levels[np.abs(levels - a[p, g]) >= 10]
            a[p, g + 8] = far[np.random.randint(len(far))]
    return np.exp2(a.ravel()).repeat(32)


BF16 = ml_dtypes.bfloat16


def bf(x):
    return np.asarray(x, np.float32).astype(BF16)


def f64(x):
    return np.asarray(x).astype(np.float64)


E2M1 = np.array([0.0, 0.5, 1.0, 1.5, 2.0, 3.0, 4.0, 6.0, -0.0, -0.5, -1.0, -1.5, -2.0, -3.0, -4.0, -6.0])


def pack_weight(w, fmt):
    k, n = w.shape
    w = f64(bf(w)).reshape(k // 32, 32, n)
    amax = np.abs(w).max(1)
    if fmt == "e4m3":
        byte = np.frexp(amax)[1] - 1 + 127 - 7
    else:
        mant, ex = np.frexp(amax / 6.0)
        byte = np.where(mant > 0.5, ex, ex - 1) + 127
    byte = np.clip(np.where(amax > 0, byte, 1), 1, 254)
    scaled = (w * np.exp2(127.0 - byte)[:, None, :]).reshape(k, n).astype(np.float32)
    by_word = np.ascontiguousarray(scaled.reshape(k // 512, 128, 4, n).transpose(0, 1, 3, 2))
    if fmt == "e4m3":
        words = by_word.astype(ml_dtypes.float8_e4m3fn).view(np.uint8)
    else:
        c = by_word.astype(ml_dtypes.float4_e2m1fn).view(np.uint8) & 0xF
        words = c[..., 0::2] | (c[..., 1::2] << 4)
    return np.ascontiguousarray(words), np.ascontiguousarray(byte.astype(np.uint8).reshape(k // 512, 16, n))


def unpack_weight(words, scales, fmt):
    g, p, n, _ = words.shape
    if fmt == "e4m3":
        vals = np.ascontiguousarray(words).view(ml_dtypes.float8_e4m3fn).astype(np.float64)
    else:
        nib = np.empty((g, p, n, 4), np.uint8)
        nib[..., 0::2] = words & 0xF
        nib[..., 1::2] = words >> 4
        vals = E2M1[nib]
    vals = vals * np.repeat(np.exp2(scales.astype(np.float64) - 127.0), 8, axis=1)[..., None]
    return vals.transpose(0, 1, 3, 2).reshape(g * 512, n)


E, F, H, MID, OUT = 128, 256, 768, 4096, 2048
D = 2 * (F + H)
IN = D + 1
FMT = "e4m3"


def setup_inputs():
    s = mx_kscale(D)
    t = mx_kscale(MID)
    w1 = np.concatenate([np.random.standard_normal((MID, D)) / np.sqrt(D) / s[None, :],
                         np.random.standard_normal((MID, 1)) * 0.5], axis=1) * t[:, None]
    dst_node_feat = bf(np.random.standard_normal((E, F)) * s[:F])
    dst_node_hidden = bf(np.random.standard_normal((E, H)) * s[F:F + H])
    src_node_feat = bf(np.random.standard_normal((E, F)) * s[F + H:2 * F + H])
    src_node_hidden = bf(np.random.standard_normal((E, H)) * s[2 * F + H:])
    edge_feat = bf(np.random.standard_normal(E))
    b1 = bf(np.random.standard_normal(MID) * 0.3 * t)
    w2 = np.random.standard_normal((OUT, MID)) / np.sqrt(MID) / t[None, :]
    w2_words, w2_scales = pack_weight(np.ascontiguousarray(w2.T), FMT)
    b2 = bf(np.random.standard_normal(OUT) * 0.3)
    return {"dst_node_feat": dst_node_feat,
            "dst_node_hidden": dst_node_hidden,
            "src_node_feat": src_node_feat,
            "src_node_hidden": src_node_hidden,
            "edge_feat": edge_feat,
            "W1": bf(w1),
            "b1": b1,
            "W2_words": w2_words,
            "W2_scales": w2_scales,
            "b2": b2}


def reference(dst_node_feat, dst_node_hidden, src_node_feat, src_node_hidden, edge_feat, W1, b1, W2_words, W2_scales, b2):
    x = np.concatenate([f64(dst_node_feat), f64(dst_node_hidden), f64(src_node_feat), f64(src_node_hidden),
                        f64(edge_feat)[:, None]], axis=1)
    w1 = f64(W1)
    pre = (mxq(x[:, :D], 1, "e4m3") @ mxq(w1[:, :D], 1, "e4m3").T) + x[:, D:] * w1[:, D] + f64(b1)
    h = np.maximum(pre, 0.0)
    return np.tanh((mxq(h, 1, "e4m3") @ unpack_weight(W2_words, W2_scales, FMT)) + f64(b2))

@@ -1,0 +1,332 @@
+from contextlib import ExitStack
+
+import concourse.mybir as mybir
+from concourse.masks import make_identity
+
+F32 = mybir.dt.float32
+BF16 = mybir.dt.bfloat16
+I32 = mybir.dt.int32
+U32 = mybir.dt.uint32
+U8 = mybir.dt.uint8
+FP8X4 = mybir.dt.float8_e4m3fn_x4
+ADD = mybir.AluOpType.add
+MULT = mybir.AluOpType.mult
+MAX = mybir.AluOpType.max
+ACT = mybir.ActivationFunctionType
+
+P = 128
+E = 128
+D = 2048
+MID = 4096
+OUT = 2048
+G = MID // 512
+UNITS = 2 * G
+ROW_PITCH = 2064
+SLOTS = 14
+SPLIT_UNITS = 3
+
+FLOPS = 2 * E * (D + 1) * MID + 2 * E * MID * OUT
+
+
+def tile_edgenetwork_w_kernel(
+    tc,
+    dst_node_feat,
+    dst_node_hidden,
+    src_node_feat,
+    src_node_hidden,
+    edge_feat,
+    W1,
+    b1,
+    W2_words,
+    W2_scales,
+    b2,
+    out,
+):
+    nc = tc.nc
+    with ExitStack() as ctx:
+        ctx.enter_context(tc.manual_schedule())
+        const = ctx.enter_context(tc.tile_pool(name="const", bufs=1))
+        big = ctx.enter_context(tc.tile_pool(name="big", bufs=SLOTS))
+        work = ctx.enter_context(tc.tile_pool(name="work", bufs=3))
+        small = ctx.enter_context(tc.tile_pool(name="small", bufs=2))
+        fin = ctx.enter_context(tc.tile_pool(name="fin", bufs=4))
+        psum = ctx.enter_context(tc.psum_pool(name="psum", bufs=6))
+
+        w1_view = W1.rearrange("(g p j) k -> g p j k", g=G, p=P, j=4)
+
+        raw = {}
+        banks = {}
+        grouped = {}
+        codes = {}
+        planes1 = {}
+        hidden = {}
+        addend = {}
+        pre = {}
+        h_grouped = {}
+        w2_tiles = {}
+
+        def load_unit(s):
+            r = big.tile([P, 2, ROW_PITCH], BF16, name="raw", tag="big", align_bytes=64)
+            g, jh = s // 2, s % 2
+            if s < SPLIT_UNITS:
+                for jj in range(2):
+                    nc.sync.dma_start(out=r[:, jj, 0:1024], in_=w1_view[g][:, 2 * jh + jj, 0:1024])
+                    nc.sync.dma_start(out=r[:, jj, 1024 : D + 1], in_=w1_view[g][:, 2 * jh + jj, 1024 : D + 1])
+            else:
+                nc.sync.dma_start(out=r[:, :, 0 : D + 1], in_=w1_view[g][:, 2 * jh : 2 * jh + 2, :])
+            raw[s] = r
+
+        def load_w2(g):
+            w = big.tile([P, OUT], U32, name="w2", tag="big", align_bytes=64)
+            src = W2_words[g].rearrange("p n t -> p (n t)").bitcast(I32)
+            if g < G - 1:
+                nc.sync.dma_start(out=w[:].bitcast(I32), in_=src)
+            else:
+                for nq in range(4):
+                    cols = slice(nq * 512, (nq + 1) * 512)
+                    nc.sync.dma_start(out=w[:, cols].bitcast(I32), in_=src[:, cols])
+            w2_tiles[g] = w
+
+        ident = const.tile([P, P], F32, name="ident")
+        make_identity(nc, ident[:])
+        warm_in = const.tile([P, 1], F32, name="warm_in")
+        warm_out = const.tile([P, 1], F32, name="warm_out")
+        nc.vector.memset(warm_in[:], 0.0)
+        nc.scalar.activation(out=warm_out[:], in_=warm_in[:], func=ACT.Tanh)
+
+        b1_rows = const.tile([P, 512], BF16, name="b1_rows")
+        nc.vector.memset(b1_rows[:].bitcast(I32), 0)
+        row = const.tile([P, OUT + E], BF16, name="row")
+        nc.vector.memset(row[:].bitcast(I32), 0)
+        ones = const.tile([P, P], BF16, name="ones")
+        nc.vector.memset(ones[:], 1.0)
+        w2_planes = const.tile([P, 2, OUT], U8, name="w2_planes", align_bytes=64)
+        nc.vector.memset(w2_planes[:].bitcast(I32), 0)
+
+        load_unit(0)
+        nc.scalar.dma_start(out=b1_rows[0:G, :], in_=b1.rearrange("(g c) -> g c", g=G))
+        nc.scalar.dma_start(out=row[0:1, OUT : OUT + E], in_=edge_feat.rearrange("(o n) -> o n", o=1))
+        nc.scalar.dma_start(out=row[0:1, 0:OUT], in_=b2.rearrange("(o n) -> o n", o=1))
+
+        x_raw = const.tile([P, D], BF16, name="x_raw")
+        nc.sync.dma_start(out=x_raw[:, 0:256], in_=dst_node_feat)
+        nc.sync.dma_start(out=x_raw[:, 256:1024], in_=dst_node_hidden)
+        nc.sync.dma_start(out=x_raw[:, 1024:1280], in_=src_node_feat)
+        nc.sync.dma_start(out=x_raw[:, 1280:2048], in_=src_node_hidden)
+        loads = [("w1", s) for s in range(1, UNITS)] + [("w2", g) for g in range(G)]
+
+        def issue(load):
+            kind, index = load
+            if kind == "w1":
+                load_unit(index)
+            else:
+                if index == 0:
+                    for a in range(2):
+                        for q in range(4):
+                            nc.sync.dma_start(
+                                out=w2_planes[32 * q : 32 * q + 16, a, :].bitcast(I32),
+                                in_=W2_scales[4 * a : 4 * a + 4, 4 * q : 4 * q + 4, :].bitcast(I32),
+                            )
+                load_w2(index)
+
+        for i in range(SLOTS - 1):
+            issue(loads[i])
+
+        b1_f32 = const.tile([P, 4, P], F32, name="b1_f32")
+        nc.vector.tensor_copy(out=b1_f32[:], in_=b1_rows[:].rearrange("r (p j) -> r j p", j=4))
+
+        w1_edge = const.tile([P, G, 4], F32, name="w1_edge")
+        b1_col = const.tile([P, G, 4], F32, name="b1_col")
+        edge_all = const.tile([P, E], F32, name="edge_all")
+        b2_all = const.tile([P, OUT], BF16, name="b2_all")
+        x_grouped = const.tile([P, D], BF16, name="x_grouped", align_bytes=64)
+        x_codes = const.tile([P, D // 4], U32, name="x_codes", align_bytes=64)
+        x_planes = const.tile([P, D // 4], U8, name="x_planes", align_bytes=64)
+        h_codes = const.tile([P, G, E], U32, name="h_codes", align_bytes=64)
+        h_planes = const.tile([P, G, E], U8, name="h_planes", align_bytes=64)
+
+        def transpose_words(src_words, first_pass):
+            bank = psum.tile([P, 512], F32, name="tp", tag="tp")
+            for cc in range(2):
+                for u in range(2):
+                    first = 256 * (first_pass + cc)
+                    nc.tensor.transpose(
+                        bank[:, (2 * cc + u) * P : (2 * cc + u + 1) * P],
+                        src_words[:, first + u : first + 256 : 2],
+                        ident[:],
+                    )
+            return bank
+
+        def copy_out(engine_is_vector, dst_words, bank):
+            src = bank[:].rearrange("w (c u p) -> w c p u", c=2, u=2, p=P)
+            if engine_is_vector:
+                nc.vector.tensor_copy(out=dst_words, in_=src)
+            else:
+                nc.scalar.copy(out=dst_words, in_=src)
+
+        def transposes(s):
+            banks[s] = [
+                transpose_words(raw[s][:, b // 2, 0:D].bitcast(F32), 2 * (b % 2)) for b in range(4)
+            ]
+
+        def edge_column(s):
+            g, jh = s // 2, s % 2
+            nc.vector.tensor_copy(out=w1_edge[:, g, 2 * jh : 2 * jh + 2], in_=raw[s][:, :, D])
+
+        def copies(s):
+            gr = work.tile([P, 4096], BF16, name="grouped", tag="grouped", align_bytes=64)
+            grouped[s] = gr
+            words = gr[:].bitcast(F32).rearrange("w (o p u) -> w o p u", o=8, p=P, u=2)
+            for b in range(4):
+                copy_out(False, words[:, 2 * b : 2 * b + 2], banks[s][b])
+
+        def quantise(s):
+            c = work.tile([P, 1024], U32, name="codes", tag="codes", align_bytes=64)
+            pl = work.tile([P, 1024], U8, name="planes", tag="planes", align_bytes=64)
+            nc.vector.quantize_mx(out=c[:].bitcast(FP8X4), scales=pl[:], in_=grouped[s][:])
+            codes[s] = c
+            planes1[s] = pl
+
+        def layer1(s):
+            g, jh = s // 2, s % 2
+            if jh == 0:
+                hidden[g] = psum.tile([P, 512], F32, name="hp", tag="hp", bufs=2)
+            for jj in range(2):
+                j = 2 * jh + jj
+                for c in range(4):
+                    o = 4 * jj + c
+                    nc.tensor.matmul_mx(
+                        out=hidden[g][:, j * E : (j + 1) * E],
+                        lhsT=codes[s][:, o * P : (o + 1) * P].bitcast(FP8X4),
+                        lhsT_scale=planes1[s][:, o * P : (o + 1) * P],
+                        rhs=x_codes[:, c * E : (c + 1) * E].bitcast(FP8X4),
+                        rhs_scale=x_planes[:, c * E : (c + 1) * E],
+                        start=(c == 0),
+                        stop=(c == 3),
+                    )
+
+        def make_addend(g):
+            a = small.tile([P, 4, E], F32, name="addend", tag="addend")
+            for j in range(4):
+                nc.vector.tensor_scalar(
+                    out=a[:, j, :],
+                    in0=edge_all[:],
+                    scalar1=w1_edge[:, g, j : j + 1],
+                    scalar2=b1_col[:, g, j : j + 1],
+                    op0=MULT,
+                    op1=ADD,
+                )
+            addend[g] = a
+
+        def add_terms(g):
+            z = small.tile([P, E, 4], F32, name="pre", tag="pre")
+            nc.vector.tensor_tensor(
+                out=z[:],
+                in0=hidden[g][:].rearrange("p (j e) -> p e j", j=4),
+                in1=addend[g][:].rearrange("p j e -> p e j"),
+                op=ADD,
+            )
+            pre[g] = z
+
+        def relu(g):
+            hg = small.tile([P, 4 * E], BF16, name="h_grouped", tag="h_grouped", align_bytes=64)
+            nc.vector.tensor_scalar(
+                out=hg[:], in0=pre[g][:].rearrange("p e j -> p (e j)"), scalar1=0.0, scalar2=None, op0=MAX
+            )
+            h_grouped[g] = hg
+
+        def quantise_h(g):
+            nc.vector.quantize_mx(
+                out=h_codes[:, g, :].bitcast(FP8X4), scales=h_planes[:, g, :], in_=h_grouped[g][:]
+            )
+
+        transposes(0)
+        copies(0)
+        edge_column(0)
+
+        x_words = x_raw[:].bitcast(F32)
+        x_out = x_grouped[:].bitcast(F32).rearrange("w (c e u) -> w c e u", c=4, e=E, u=2)
+        x_bank0 = transpose_words(x_words, 0)
+        x_bank1 = transpose_words(x_words, 2)
+        copy_out(False, x_out[:, 0:2], x_bank0)
+        copy_out(True, x_out[:, 2:4], x_bank1)
+
+        edge_bank = psum.tile([P, 512], F32, name="edge_bank", tag="tp")
+        nc.tensor.matmul(edge_bank[:, 0:E], lhsT=ones[:], rhs=row[:, OUT : OUT + E], start=True, stop=True)
+        b1_bank = psum.tile([P, 512], F32, name="b1_bank", tag="tp")
+        for j in range(4):
+            nc.tensor.transpose(b1_bank[:, j * P : (j + 1) * P], b1_f32[:, j, :], ident[:])
+        nc.vector.tensor_copy(out=edge_all[:], in_=edge_bank[:, 0:E])
+        nc.vector.tensor_copy(
+            out=b1_col[:].rearrange("p g j -> p j g"),
+            in_=b1_bank[:].rearrange("p (j r) -> p j r", j=4)[:, :, 0:G],
+        )
+        nc.vector.quantize_mx(out=x_codes[:].bitcast(FP8X4), scales=x_planes[:], in_=x_grouped[:])
+        for half in range(2):
+            b2_bank = psum.tile([P, 1024], BF16, name="b2_bank", tag="tp")
+            for i in range(2):
+                first = 1024 * half + 512 * i
+                nc.tensor.matmul(
+                    b2_bank[:, 512 * i : 512 * (i + 1)],
+                    lhsT=ones[:],
+                    rhs=row[:, first : first + 512],
+                    start=True,
+                    stop=True,
+                )
+            nc.scalar.copy(out=b2_all[:, 1024 * half : 1024 * (half + 1)], in_=b2_bank[:])
+
+        acc = []
+
+        def layer2(g):
+            if g == 0:
+                for nq in range(4):
+                    acc.append(psum.tile([P, 512], F32, name="acc%d" % nq, tag="tp"))
+            a, b = g // 4, g % 4
+            for nq in range(4):
+                cols = slice(nq * 512, (nq + 1) * 512)
+                nc.tensor.matmul_mx(
+                    out=acc[nq][:],
+                    lhsT=h_codes[:, g, :].bitcast(FP8X4),
+                    lhsT_scale=h_planes[:, g, :],
+                    rhs=w2_tiles[g][:, cols].bitcast(FP8X4),
+                    rhs_scale=w2_planes[4 * b : P, a, cols],
+                    start=(g == 0),
+                    stop=(g == G - 1),
+                )
+
+        position = SLOTS - 1
+        for s in range(1, UNITS + 4):
+            if s < UNITS:
+                transposes(s)
+                copies(s)
+            if s >= 4 and s % 2 == 0:
+                add_terms((s - 4) // 2)
+                relu((s - 4) // 2)
+            if s < UNITS:
+                edge_column(s)
+            if s - 1 < UNITS:
+                quantise(s - 1)
+            if s >= 5 and s % 2 == 1:
+                quantise_h((s - 5) // 2)
+            if s >= 3 and s % 2 == 1 and (s - 3) // 2 < G:
+                make_addend((s - 3) // 2)
+            if 0 <= s - 2 < UNITS:
+                layer1(s - 2)
+            if s == UNITS:
+                layer2(0)
+            if s == UNITS + 1:
+                layer2(1)
+                layer2(2)
+            if position < len(loads):
+                issue(loads[position])
+                position += 1
+
+        for g in range(3, G):
+            layer2(g)
+        for nq in range(4):
+            cols = slice(nq * 512, (nq + 1) * 512)
+            biased = fin.tile([P, 512], F32, name="biased", tag="biased")
+            nc.vector.tensor_tensor(out=biased[:], in0=acc[nq][:], in1=b2_all[:, cols], op=ADD)
+            result = fin.tile([P, 512], F32, name="result", tag="result")
+            nc.scalar.activation(out=result[:], in_=biased[:], func=ACT.Tanh)
+            nc.sync.dma_start(out=out[:, cols], in_=result[:])

@@ -21,7 +21,7 @@ MID = 4096
 OUT = 2048
 G = MID // 512
 UNITS = 2 * G
-ROW_PITCH = 2064
+ROW = D + 1
 SLOTS = 14
 SPLIT_UNITS = 3
 
@@ -52,9 +52,10 @@ def tile_edgenetwork_w_kernel(
         fin = ctx.enter_context(tc.tile_pool(name="fin", bufs=4))
         psum = ctx.enter_context(tc.psum_pool(name="psum", bufs=6))
 
-        w1_view = W1.rearrange("(g p j) k -> g p j k", g=G, p=P, j=4)
+        w1_view = W1.rearrange("(g p h j) k -> g p h (j k)", g=G, p=P, h=2, j=2)
 
         raw = {}
+        aligned = {}
         banks = {}
         grouped = {}
         codes = {}
@@ -66,14 +67,13 @@ def tile_edgenetwork_w_kernel(
         w2_tiles = {}
 
         def load_unit(s):
-            r = big.tile([P, 2, ROW_PITCH], BF16, name="raw", tag="big", align_bytes=64)
+            r = big.tile([P, 2 * ROW], BF16, name="raw", tag="big", align_bytes=64)
             g, jh = s // 2, s % 2
             if s < SPLIT_UNITS:
-                for jj in range(2):
-                    nc.sync.dma_start(out=r[:, jj, 0:1024], in_=w1_view[g][:, 2 * jh + jj, 0:1024])
-                    nc.sync.dma_start(out=r[:, jj, 1024 : D + 1], in_=w1_view[g][:, 2 * jh + jj, 1024 : D + 1])
+                for lo, hi in ((0, 1024), (1024, 2048), (2048, 3072), (3072, 2 * ROW)):
+                    nc.sync.dma_start(out=r[:, lo:hi], in_=w1_view[g][:, jh, lo:hi])
             else:
-                nc.sync.dma_start(out=r[:, :, 0 : D + 1], in_=w1_view[g][:, 2 * jh : 2 * jh + 2, :])
+                nc.sync.dma_start(out=r[:], in_=w1_view[g][:, jh, :])
             raw[s] = r
 
         def load_w2(g):
@@ -145,14 +145,19 @@ def tile_edgenetwork_w_kernel(
         h_codes = const.tile([P, G, E], U32, name="h_codes", align_bytes=64)
         h_planes = const.tile([P, G, E], U8, name="h_planes", align_bytes=64)
 
-        def transpose_words(src_words, first_pass):
+        def transpose_words(src_words, first_pass, split):
             bank = psum.tile([P, 512], F32, name="tp", tag="tp")
             for cc in range(2):
                 for u in range(2):
-                    first = 256 * (first_pass + cc)
+                    if split:
+                        first = 512 * u + P * (first_pass + cc)
+                        words = src_words[:, first : first + P]
+                    else:
+                        first = 256 * (first_pass + cc)
+                        words = src_words[:, first + u : first + 256 : 2]
                     nc.tensor.transpose(
                         bank[:, (2 * cc + u) * P : (2 * cc + u + 1) * P],
-                        src_words[:, first + u : first + 256 : 2],
+                        words,
                         ident[:],
                     )
             return bank
@@ -165,13 +170,26 @@ def tile_edgenetwork_w_kernel(
                 nc.scalar.copy(out=dst_words, in_=src)
 
         def transposes(s):
+            first_row = raw[s][:, 0:D].bitcast(F32)
+            second_row = aligned[s][:].bitcast(F32)
             banks[s] = [
-                transpose_words(raw[s][:, b // 2, 0:D].bitcast(F32), 2 * (b % 2)) for b in range(4)
+                transpose_words(first_row, 0, False),
+                transpose_words(first_row, 2, False),
+                transpose_words(second_row, 0, True),
+                transpose_words(second_row, 2, True),
             ]
+
+        def align(s):
+            t = work.tile([P, D], BF16, name="aligned", tag="aligned", align_bytes=64)
+            nc.vector.tensor_copy(
+                out=t[:].rearrange("p (u w e) -> p u w e", u=2, e=2),
+                in_=raw[s][:, ROW : ROW + D].rearrange("p (w u e) -> p u w e", u=2, e=2),
+            )
+            aligned[s] = t
 
         def edge_column(s):
             g, jh = s // 2, s % 2
-            nc.vector.tensor_copy(out=w1_edge[:, g, 2 * jh : 2 * jh + 2], in_=raw[s][:, :, D])
+            nc.vector.tensor_copy(out=w1_edge[:, g, 2 * jh : 2 * jh + 2], in_=raw[s][:, D : 2 * ROW : ROW])
 
         def copies(s):
             gr = work.tile([P, 4096], BF16, name="grouped", tag="grouped", align_bytes=64)
@@ -240,14 +258,15 @@ def tile_edgenetwork_w_kernel(
                 out=h_codes[:, g, :].bitcast(FP8X4), scales=h_planes[:, g, :], in_=h_grouped[g][:]
             )
 
+        align(0)
         transposes(0)
         copies(0)
         edge_column(0)
 
         x_words = x_raw[:].bitcast(F32)
         x_out = x_grouped[:].bitcast(F32).rearrange("w (c e u) -> w c e u", c=4, e=E, u=2)
-        x_bank0 = transpose_words(x_words, 0)
-        x_bank1 = transpose_words(x_words, 2)
+        x_bank0 = transpose_words(x_words, 0, False)
+        x_bank1 = transpose_words(x_words, 2, False)
         copy_out(False, x_out[:, 0:2], x_bank0)
         copy_out(True, x_out[:, 2:4], x_bank1)
 
@@ -275,6 +294,7 @@ def tile_edgenetwork_w_kernel(
                 )
             nc.scalar.copy(out=b2_all[:, 1024 * half : 1024 * (half + 1)], in_=b2_bank[:])
 
+        align(1)
         acc = []
 
         def layer2(g):
@@ -310,6 +330,8 @@ def tile_edgenetwork_w_kernel(
                 quantise_h((s - 5) // 2)
             if s >= 3 and s % 2 == 1 and (s - 3) // 2 < G:
                 make_addend((s - 3) // 2)
+            if s + 1 < UNITS:
+                align(s + 1)
             if 0 <= s - 2 < UNITS:
                 layer1(s - 2)
             if s == UNITS:

@@ -23,7 +23,7 @@ G = MID // 512
 UNITS = 2 * G
 ROW = D + 1
 SLOTS = 14
-SPLIT_UNITS = 3
+SPLIT_UNITS = 1
 
 FLOPS = 2 * E * (D + 1) * MID + 2 * E * MID * OUT
 
@@ -55,7 +55,7 @@ def tile_edgenetwork_w_kernel(
         w1_view = W1.rearrange("(g p h j) k -> g p h (j k)", g=G, p=P, h=2, j=2)
 
         raw = {}
-        aligned = {}
+        split = {}
         banks = {}
         grouped = {}
         codes = {}
@@ -75,6 +75,13 @@ def tile_edgenetwork_w_kernel(
             else:
                 nc.sync.dma_start(out=r[:], in_=w1_view[g][:, jh, :])
             raw[s] = r
+
+        def load_scales(i):
+            a, q = i // 4, i % 4
+            nc.sync.dma_start(
+                out=w2_planes[32 * q : 32 * q + 16, a, :].bitcast(I32),
+                in_=W2_scales[4 * a : 4 * a + 4, 4 * q : 4 * q + 4, :].bitcast(I32),
+            )
 
         def load_w2(g):
             w = big.tile([P, OUT], U32, name="w2", tag="big", align_bytes=64)
@@ -119,14 +126,9 @@ def tile_edgenetwork_w_kernel(
             kind, index = load
             if kind == "w1":
                 load_unit(index)
+                if 4 <= index < 12:
+                    load_scales(index - 4)
             else:
-                if index == 0:
-                    for a in range(2):
-                        for q in range(4):
-                            nc.sync.dma_start(
-                                out=w2_planes[32 * q : 32 * q + 16, a, :].bitcast(I32),
-                                in_=W2_scales[4 * a : 4 * a + 4, 4 * q : 4 * q + 4, :].bitcast(I32),
-                            )
                 load_w2(index)
 
         for i in range(SLOTS - 1):
@@ -139,17 +141,18 @@ def tile_edgenetwork_w_kernel(
         b1_col = const.tile([P, G, 4], F32, name="b1_col")
         edge_all = const.tile([P, E], F32, name="edge_all")
         b2_all = const.tile([P, OUT], BF16, name="b2_all")
-        x_grouped = const.tile([P, D], BF16, name="x_grouped", align_bytes=64)
-        x_codes = const.tile([P, D // 4], U32, name="x_codes", align_bytes=64)
-        x_planes = const.tile([P, D // 4], U8, name="x_planes", align_bytes=64)
+        x_split = const.tile([P, D], BF16, name="x_split", align_bytes=64)
+        x_grouped = const.tile([P, 2, D], BF16, name="x_grouped", align_bytes=64)
+        x_codes = const.tile([P, 2, D // 4], U32, name="x_codes", align_bytes=64)
+        x_planes = const.tile([P, 2, D // 4], U8, name="x_planes", align_bytes=64)
         h_codes = const.tile([P, G, E], U32, name="h_codes", align_bytes=64)
         h_planes = const.tile([P, G, E], U8, name="h_planes", align_bytes=64)
 
-        def transpose_words(src_words, first_pass, split):
+        def transpose_words(src_words, first_pass, is_split):
             bank = psum.tile([P, 512], F32, name="tp", tag="tp")
             for cc in range(2):
                 for u in range(2):
-                    if split:
+                    if is_split:
                         first = 512 * u + P * (first_pass + cc)
                         words = src_words[:, first : first + P]
                     else:
@@ -171,7 +174,7 @@ def tile_edgenetwork_w_kernel(
 
         def transposes(s):
             first_row = raw[s][:, 0:D].bitcast(F32)
-            second_row = aligned[s][:].bitcast(F32)
+            second_row = split[s][:].bitcast(F32)
             banks[s] = [
                 transpose_words(first_row, 0, False),
                 transpose_words(first_row, 2, False),
@@ -179,13 +182,16 @@ def tile_edgenetwork_w_kernel(
                 transpose_words(second_row, 2, True),
             ]
 
-        def align(s):
-            t = work.tile([P, D], BF16, name="aligned", tag="aligned", align_bytes=64)
+        def split_blocks(dst, src):
             nc.vector.tensor_copy(
-                out=t[:].rearrange("p (u w e) -> p u w e", u=2, e=2),
-                in_=raw[s][:, ROW : ROW + D].rearrange("p (w u e) -> p u w e", u=2, e=2),
+                out=dst.rearrange("p (u b e) -> p u b e", u=2, e=16),
+                in_=src.rearrange("p (b u e) -> p u b e", u=2, e=16),
             )
-            aligned[s] = t
+
+        def split_row(s):
+            t = work.tile([P, D], BF16, name="split", tag="split", align_bytes=64)
+            split_blocks(t[:], raw[s][:, ROW : ROW + D])
+            split[s] = t
 
         def edge_column(s):
             g, jh = s // 2, s % 2
@@ -217,8 +223,8 @@ def tile_edgenetwork_w_kernel(
                         out=hidden[g][:, j * E : (j + 1) * E],
                         lhsT=codes[s][:, o * P : (o + 1) * P].bitcast(FP8X4),
                         lhsT_scale=planes1[s][:, o * P : (o + 1) * P],
-                        rhs=x_codes[:, c * E : (c + 1) * E].bitcast(FP8X4),
-                        rhs_scale=x_planes[:, c * E : (c + 1) * E],
+                        rhs=x_codes[:, jj, c * E : (c + 1) * E].bitcast(FP8X4),
+                        rhs_scale=x_planes[:, jj, c * E : (c + 1) * E],
                         start=(c == 0),
                         stop=(c == 3),
                     )
@@ -258,17 +264,25 @@ def tile_edgenetwork_w_kernel(
                 out=h_codes[:, g, :].bitcast(FP8X4), scales=h_planes[:, g, :], in_=h_grouped[g][:]
             )
 
-        align(0)
+        split_row(0)
+        split_blocks(x_split[:], x_raw[:])
         transposes(0)
         copies(0)
         edge_column(0)
-
-        x_words = x_raw[:].bitcast(F32)
-        x_out = x_grouped[:].bitcast(F32).rearrange("w (c e u) -> w c e u", c=4, e=E, u=2)
-        x_bank0 = transpose_words(x_words, 0, False)
-        x_bank1 = transpose_words(x_words, 2, False)
-        copy_out(False, x_out[:, 0:2], x_bank0)
-        copy_out(True, x_out[:, 2:4], x_bank1)
+        x_banks = [
+            transpose_words((x_raw, x_split)[o][:].bitcast(F32), first_pass, o == 1)
+            for o in range(2)
+            for first_pass in (0, 2)
+        ]
+        split_row(1)
+        for o in range(2):
+            x_out = x_grouped[:, o, :].bitcast(F32).rearrange("w (c e u) -> w c e u", c=4, e=E, u=2)
+            copy_out(False, x_out[:, 0:2], x_banks[2 * o])
+            copy_out(True, x_out[:, 2:4], x_banks[2 * o + 1])
+        for o in range(2):
+            nc.vector.quantize_mx(
+                out=x_codes[:, o, :].bitcast(FP8X4), scales=x_planes[:, o, :], in_=x_grouped[:, o, :]
+            )
 
         edge_bank = psum.tile([P, 512], F32, name="edge_bank", tag="tp")
         nc.tensor.matmul(edge_bank[:, 0:E], lhsT=ones[:], rhs=row[:, OUT : OUT + E], start=True, stop=True)
@@ -280,21 +294,21 @@ def tile_edgenetwork_w_kernel(
             out=b1_col[:].rearrange("p g j -> p j g"),
             in_=b1_bank[:].rearrange("p (j r) -> p j r", j=4)[:, :, 0:G],
         )
-        nc.vector.quantize_mx(out=x_codes[:].bitcast(FP8X4), scales=x_planes[:], in_=x_grouped[:])
-        for half in range(2):
-            b2_bank = psum.tile([P, 1024], BF16, name="b2_bank", tag="tp")
-            for i in range(2):
-                first = 1024 * half + 512 * i
-                nc.tensor.matmul(
-                    b2_bank[:, 512 * i : 512 * (i + 1)],
-                    lhsT=ones[:],
-                    rhs=row[:, first : first + 512],
-                    start=True,
-                    stop=True,
-                )
-            nc.scalar.copy(out=b2_all[:, 1024 * half : 1024 * (half + 1)], in_=b2_bank[:])
 
-        align(1)
+        def spread_b2():
+            for half in range(2):
+                b2_bank = psum.tile([P, 1024], BF16, name="b2_bank", tag="tp")
+                for i in range(2):
+                    first = 1024 * half + 512 * i
+                    nc.tensor.matmul(
+                        b2_bank[:, 512 * i : 512 * (i + 1)],
+                        lhsT=ones[:],
+                        rhs=row[:, first : first + 512],
+                        start=True,
+                        stop=True,
+                    )
+                nc.scalar.copy(out=b2_all[:, 1024 * half : 1024 * (half + 1)], in_=b2_bank[:])
+
         acc = []
 
         def layer2(g):
@@ -331,10 +345,11 @@ def tile_edgenetwork_w_kernel(
             if s >= 3 and s % 2 == 1 and (s - 3) // 2 < G:
                 make_addend((s - 3) // 2)
             if s + 1 < UNITS:
-                align(s + 1)
+                split_row(s + 1)
             if 0 <= s - 2 < UNITS:
                 layer1(s - 2)
             if s == UNITS:
+                spread_b2()
                 layer2(0)
             if s == UNITS + 1:
                 layer2(1)

@@ -22,8 +22,10 @@ OUT = 2048
 G = MID // 512
 UNITS = 2 * G
 ROW = D + 1
-SLOTS = 14
+W1_SLOTS = 8
+W2_SLOTS = 12
 SPLIT_UNITS = 1
+HALF = OUT // 2
 
 FLOPS = 2 * E * (D + 1) * MID + 2 * E * MID * OUT
 
@@ -46,11 +48,12 @@ def tile_edgenetwork_w_kernel(
     with ExitStack() as ctx:
         ctx.enter_context(tc.manual_schedule())
         const = ctx.enter_context(tc.tile_pool(name="const", bufs=1))
-        big = ctx.enter_context(tc.tile_pool(name="big", bufs=SLOTS))
+        big = ctx.enter_context(tc.tile_pool(name="big", bufs=W1_SLOTS))
+        w2_pool = ctx.enter_context(tc.tile_pool(name="w2_pool", bufs=W2_SLOTS))
         work = ctx.enter_context(tc.tile_pool(name="work", bufs=3))
         small = ctx.enter_context(tc.tile_pool(name="small", bufs=2))
         fin = ctx.enter_context(tc.tile_pool(name="fin", bufs=4))
-        psum = ctx.enter_context(tc.psum_pool(name="psum", bufs=6))
+        psum = ctx.enter_context(tc.psum_pool(name="psum", bufs=4))
 
         w1_view = W1.rearrange("(g p h j) k -> g p h (j k)", g=G, p=P, h=2, j=2)
 
@@ -83,16 +86,17 @@ def tile_edgenetwork_w_kernel(
                 in_=W2_scales[4 * a : 4 * a + 4, 4 * q : 4 * q + 4, :].bitcast(I32),
             )
 
-        def load_w2(g):
-            w = big.tile([P, OUT], U32, name="w2", tag="big", align_bytes=64)
+        def load_w2(half, g):
+            w = w2_pool.tile([P, HALF], U32, name="w2", tag="w2", align_bytes=64)
             src = W2_words[g].rearrange("p n t -> p (n t)").bitcast(I32)
-            if g < G - 1:
-                nc.sync.dma_start(out=w[:].bitcast(I32), in_=src)
-            else:
-                for nq in range(4):
-                    cols = slice(nq * 512, (nq + 1) * 512)
-                    nc.sync.dma_start(out=w[:, cols].bitcast(I32), in_=src[:, cols])
-            w2_tiles[g] = w
+            pieces = 2 if (half, g) == (1, G - 1) else 1
+            width = HALF // pieces
+            for i in range(pieces):
+                nc.sync.dma_start(
+                    out=w[:, i * width : (i + 1) * width].bitcast(I32),
+                    in_=src[:, half * HALF + i * width : half * HALF + (i + 1) * width],
+                )
+            w2_tiles[half, g] = w
 
         ident = const.tile([P, P], F32, name="ident")
         make_identity(nc, ident[:])
@@ -115,28 +119,23 @@ def tile_edgenetwork_w_kernel(
         nc.scalar.dma_start(out=row[0:1, OUT : OUT + E], in_=edge_feat.rearrange("(o n) -> o n", o=1))
         nc.scalar.dma_start(out=row[0:1, 0:OUT], in_=b2.rearrange("(o n) -> o n", o=1))
 
+        def load_next(s):
+            load_unit(s)
+            if 4 <= s < 12:
+                load_scales(s - 4)
+            if 8 <= s < 12:
+                load_w2(0, s - 8)
+
+        load_next(1)
         x_raw = const.tile([P, D], BF16, name="x_raw")
         nc.sync.dma_start(out=x_raw[:, 0:256], in_=dst_node_feat)
         nc.sync.dma_start(out=x_raw[:, 256:1024], in_=dst_node_hidden)
         nc.sync.dma_start(out=x_raw[:, 1024:1280], in_=src_node_feat)
         nc.sync.dma_start(out=x_raw[:, 1280:2048], in_=src_node_hidden)
-        loads = [("w1", s) for s in range(1, UNITS)] + [("w2", g) for g in range(G)]
-
-        def issue(load):
-            kind, index = load
-            if kind == "w1":
-                load_unit(index)
-                if 4 <= index < 12:
-                    load_scales(index - 4)
-            else:
-                load_w2(index)
-
-        for i in range(SLOTS - 1):
-            issue(loads[i])
+        for s in range(2, W1_SLOTS):
+            load_next(s)
 
         b1_f32 = const.tile([P, 4, P], F32, name="b1_f32")
-        nc.vector.tensor_copy(out=b1_f32[:], in_=b1_rows[:].rearrange("r (p j) -> r j p", j=4))
-
         w1_edge = const.tile([P, G, 4], F32, name="w1_edge")
         b1_col = const.tile([P, G, 4], F32, name="b1_col")
         edge_all = const.tile([P, E], F32, name="edge_all")
@@ -148,8 +147,8 @@ def tile_edgenetwork_w_kernel(
         h_codes = const.tile([P, G, E], U32, name="h_codes", align_bytes=64)
         h_planes = const.tile([P, G, E], U8, name="h_planes", align_bytes=64)
 
-        def transpose_words(src_words, first_pass, is_split):
-            bank = psum.tile([P, 512], F32, name="tp", tag="tp")
+        def transpose_words(src_words, first_pass, is_split, tag="tp"):
+            bank = psum.tile([P, 512], F32, name=tag, tag=tag, bufs=4 if tag == "tp" else 2)
             for cc in range(2):
                 for u in range(2):
                     if is_split:
@@ -195,7 +194,7 @@ def tile_edgenetwork_w_kernel(
 
         def edge_column(s):
             g, jh = s // 2, s % 2
-            nc.vector.tensor_copy(out=w1_edge[:, g, 2 * jh : 2 * jh + 2], in_=raw[s][:, D : 2 * ROW : ROW])
+            nc.gpsimd.tensor_copy(out=w1_edge[:, g, 2 * jh : 2 * jh + 2], in_=raw[s][:, D : 2 * ROW : ROW])
 
         def copies(s):
             gr = work.tile([P, 4096], BF16, name="grouped", tag="grouped", align_bytes=64)
@@ -265,39 +264,38 @@ def tile_edgenetwork_w_kernel(
             )
 
         split_row(0)
-        split_blocks(x_split[:], x_raw[:])
         transposes(0)
         copies(0)
         edge_column(0)
-        x_banks = [
-            transpose_words((x_raw, x_split)[o][:].bitcast(F32), first_pass, o == 1)
-            for o in range(2)
-            for first_pass in (0, 2)
-        ]
         split_row(1)
-        for o in range(2):
-            x_out = x_grouped[:, o, :].bitcast(F32).rearrange("w (c e u) -> w c e u", c=4, e=E, u=2)
-            copy_out(False, x_out[:, 0:2], x_banks[2 * o])
-            copy_out(True, x_out[:, 2:4], x_banks[2 * o + 1])
-        for o in range(2):
-            nc.vector.quantize_mx(
-                out=x_codes[:, o, :].bitcast(FP8X4), scales=x_planes[:, o, :], in_=x_grouped[:, o, :]
-            )
+        split_blocks(x_split[:], x_raw[:])
+        nc.vector.tensor_copy(out=b1_f32[:], in_=b1_rows[:].rearrange("r (p j) -> r j p", j=4))
 
-        edge_bank = psum.tile([P, 512], F32, name="edge_bank", tag="tp")
-        nc.tensor.matmul(edge_bank[:, 0:E], lhsT=ones[:], rhs=row[:, OUT : OUT + E], start=True, stop=True)
-        b1_bank = psum.tile([P, 512], F32, name="b1_bank", tag="tp")
-        for j in range(4):
-            nc.tensor.transpose(b1_bank[:, j * P : (j + 1) * P], b1_f32[:, j, :], ident[:])
-        nc.vector.tensor_copy(out=edge_all[:], in_=edge_bank[:, 0:E])
-        nc.vector.tensor_copy(
-            out=b1_col[:].rearrange("p g j -> p j g"),
-            in_=b1_bank[:].rearrange("p (j r) -> p j r", j=4)[:, :, 0:G],
-        )
+        def quantise_x():
+            for o, tag in enumerate(("acc", "hp")):
+                words = (x_raw, x_split)[o][:].bitcast(F32)
+                x_out = x_grouped[:, o, :].bitcast(F32).rearrange("w (c e u) -> w c e u", c=4, e=E, u=2)
+                for h in range(2):
+                    copy_out(False, x_out[:, 2 * h : 2 * h + 2], transpose_words(words, 2 * h, o == 1, tag))
+                nc.vector.quantize_mx(
+                    out=x_codes[:, o, :].bitcast(FP8X4), scales=x_planes[:, o, :], in_=x_grouped[:, o, :]
+                )
+
+        def spread_edge_and_b1():
+            edge_bank = psum.tile([P, 512], F32, name="edge_bank", tag="acc", bufs=2)
+            nc.tensor.matmul(edge_bank[:, 0:E], lhsT=ones[:], rhs=row[:, OUT : OUT + E], start=True, stop=True)
+            b1_bank = psum.tile([P, 512], F32, name="b1_bank", tag="acc", bufs=2)
+            for j in range(4):
+                nc.tensor.transpose(b1_bank[:, j * P : (j + 1) * P], b1_f32[:, j, :], ident[:])
+            nc.vector.tensor_copy(out=edge_all[:], in_=edge_bank[:, 0:E])
+            nc.vector.tensor_copy(
+                out=b1_col[:].rearrange("p g j -> p j g"),
+                in_=b1_bank[:].rearrange("p (j r) -> p j r", j=4)[:, :, 0:G],
+            )
 
         def spread_b2():
             for half in range(2):
-                b2_bank = psum.tile([P, 1024], BF16, name="b2_bank", tag="tp")
+                b2_bank = psum.tile([P, 1024], BF16, name="b2_bank", tag="tp", bufs=4)
                 for i in range(2):
                     first = 1024 * half + 512 * i
                     nc.tensor.matmul(
@@ -309,26 +307,37 @@ def tile_edgenetwork_w_kernel(
                     )
                 nc.scalar.copy(out=b2_all[:, 1024 * half : 1024 * (half + 1)], in_=b2_bank[:])
 
-        acc = []
+        acc = {}
 
-        def layer2(g):
+        def layer2(half, g):
             if g == 0:
-                for nq in range(4):
-                    acc.append(psum.tile([P, 512], F32, name="acc%d" % nq, tag="tp"))
+                tag = ("acc", "tp")[half]
+                for i in range(2):
+                    acc[half, i] = psum.tile([P, 512], F32, name=tag, tag=tag, bufs=(2, 4)[half])
             a, b = g // 4, g % 4
-            for nq in range(4):
-                cols = slice(nq * 512, (nq + 1) * 512)
+            for i in range(2):
+                cols = slice(i * 512, (i + 1) * 512)
+                scale_cols = slice(half * HALF + i * 512, half * HALF + (i + 1) * 512)
                 nc.tensor.matmul_mx(
-                    out=acc[nq][:],
+                    out=acc[half, i][:],
                     lhsT=h_codes[:, g, :].bitcast(FP8X4),
                     lhsT_scale=h_planes[:, g, :],
-                    rhs=w2_tiles[g][:, cols].bitcast(FP8X4),
-                    rhs_scale=w2_planes[4 * b : P, a, cols],
+                    rhs=w2_tiles[half, g][:, cols].bitcast(FP8X4),
+                    rhs_scale=w2_planes[4 * b : P, a, scale_cols],
                     start=(g == 0),
                     stop=(g == G - 1),
                 )
 
-        position = SLOTS - 1
+        def finish(half):
+            for i in range(2):
+                cols = slice(half * HALF + i * 512, half * HALF + (i + 1) * 512)
+                biased = fin.tile([P, 512], F32, name="biased", tag="biased")
+                nc.vector.tensor_tensor(out=biased[:], in0=acc[half, i][:], in1=b2_all[:, cols], op=ADD)
+                result = fin.tile([P, 512], F32, name="result", tag="result")
+                nc.scalar.activation(out=result[:], in_=biased[:], func=ACT.Tanh)
+                nc.sync.dma_start(out=out[:, cols], in_=result[:])
+
+        late_w2 = {8: ((0, 4), (0, 5)), 9: ((0, 6), (0, 7)), 10: ((1, 0), (1, 1)), 11: ((1, 2), (1, 3)), 12: ((1, 4), (1, 5)), 13: ((1, 6),), 14: ((1, 7),)}
         for s in range(1, UNITS + 4):
             if s < UNITS:
                 transposes(s)
@@ -338,32 +347,39 @@ def tile_edgenetwork_w_kernel(
                 relu((s - 4) // 2)
             if s < UNITS:
                 edge_column(s)
+            if s + 1 < UNITS:
+                split_row(s + 1)
             if s - 1 < UNITS:
                 quantise(s - 1)
+            if s == 1:
+                quantise_x()
+            if s == 2:
+                spread_edge_and_b1()
             if s >= 5 and s % 2 == 1:
                 quantise_h((s - 5) // 2)
             if s >= 3 and s % 2 == 1 and (s - 3) // 2 < G:
                 make_addend((s - 3) // 2)
-            if s + 1 < UNITS:
-                split_row(s + 1)
             if 0 <= s - 2 < UNITS:
                 layer1(s - 2)
+            if s >= 7 and s % 2 == 1 and (s - 7) // 2 < 5:
+                layer2(0, (s - 7) // 2)
             if s == UNITS:
                 spread_b2()
-                layer2(0)
+                layer2(0, 5)
+                layer2(1, 0)
             if s == UNITS + 1:
-                layer2(1)
-                layer2(2)
-            if position < len(loads):
-                issue(loads[position])
-                position += 1
+                for g in range(1, 4):
+                    layer2(1, g)
+            if s == UNITS + 2:
+                layer2(0, 6)
+                layer2(1, 4)
+            if s + W1_SLOTS - 1 < UNITS:
+                load_next(s + W1_SLOTS - 1)
+            for half, g in late_w2.get(s, ()):
+                load_w2(half, g)
 
-        for g in range(3, G):
-            layer2(g)
-        for nq in range(4):
-            cols = slice(nq * 512, (nq + 1) * 512)
-            biased = fin.tile([P, 512], F32, name="biased", tag="biased")
-            nc.vector.tensor_tensor(out=biased[:], in0=acc[nq][:], in1=b2_all[:, cols], op=ADD)
-            result = fin.tile([P, 512], F32, name="result", tag="result")
-            nc.scalar.activation(out=result[:], in_=biased[:], func=ACT.Tanh)
-            nc.sync.dma_start(out=out[:, cols], in_=result[:])
+        layer2(0, 7)
+        finish(0)
+        for g in range(5, G):
+            layer2(1, g)
+        finish(1)

@@ -23,9 +23,8 @@ G = MID // 512
 UNITS = 2 * G
 ROW = D + 1
 W1_SLOTS = 8
-W2_SLOTS = 12
+W2_SLOTS = 5
 SPLIT_UNITS = 1
-HALF = OUT // 2
 
 FLOPS = 2 * E * (D + 1) * MID + 2 * E * MID * OUT
 
@@ -53,9 +52,11 @@ def tile_edgenetwork_w_kernel(
         work = ctx.enter_context(tc.tile_pool(name="work", bufs=3))
         small = ctx.enter_context(tc.tile_pool(name="small", bufs=2))
         fin = ctx.enter_context(tc.tile_pool(name="fin", bufs=4))
-        psum = ctx.enter_context(tc.psum_pool(name="psum", bufs=4))
+        psum = ctx.enter_context(tc.psum_pool(name="psum", bufs=6))
 
         w1_view = W1.rearrange("(g p h j) k -> g p h (j k)", g=G, p=P, h=2, j=2)
+
+        pieces = ((0, 512), (512, 1024), (1024, 1536), (1536, 1792), (1792, OUT))
 
         raw = {}
         split = {}
@@ -86,17 +87,15 @@ def tile_edgenetwork_w_kernel(
                 in_=W2_scales[4 * a : 4 * a + 4, 4 * q : 4 * q + 4, :].bitcast(I32),
             )
 
-        def load_w2(half, g):
-            w = w2_pool.tile([P, HALF], U32, name="w2", tag="w2", align_bytes=64)
+        def load_w2(g):
+            if g < W2_SLOTS:
+                w = w2_pool.tile([P, OUT], U32, name="w2", tag="w2", align_bytes=64)
+            else:
+                w = big.tile([P, OUT], U32, name="w2_late", tag="big", align_bytes=64)
             src = W2_words[g].rearrange("p n t -> p (n t)").bitcast(I32)
-            pieces = 2 if (half, g) == (1, G - 1) else 1
-            width = HALF // pieces
-            for i in range(pieces):
-                nc.sync.dma_start(
-                    out=w[:, i * width : (i + 1) * width].bitcast(I32),
-                    in_=src[:, half * HALF + i * width : half * HALF + (i + 1) * width],
-                )
-            w2_tiles[half, g] = w
+            for lo, hi in pieces if g == G - 1 else ((0, OUT),):
+                nc.sync.dma_start(out=w[:, lo:hi].bitcast(I32), in_=src[:, lo:hi])
+            w2_tiles[g] = w
 
         ident = const.tile([P, P], F32, name="ident")
         make_identity(nc, ident[:])
@@ -121,10 +120,6 @@ def tile_edgenetwork_w_kernel(
 
         def load_next(s):
             load_unit(s)
-            if 4 <= s < 12:
-                load_scales(s - 4)
-            if 8 <= s < 12:
-                load_w2(0, s - 8)
 
         load_next(1)
         x_raw = const.tile([P, D], BF16, name="x_raw")
@@ -147,8 +142,8 @@ def tile_edgenetwork_w_kernel(
         h_codes = const.tile([P, G, E], U32, name="h_codes", align_bytes=64)
         h_planes = const.tile([P, G, E], U8, name="h_planes", align_bytes=64)
 
-        def transpose_words(src_words, first_pass, is_split, tag="tp"):
-            bank = psum.tile([P, 512], F32, name=tag, tag=tag, bufs=4 if tag == "tp" else 2)
+        def transpose_words(src_words, first_pass, is_split):
+            bank = psum.tile([P, 512], F32, name="tp", tag="tp")
             for cc in range(2):
                 for u in range(2):
                     if is_split:
@@ -242,7 +237,7 @@ def tile_edgenetwork_w_kernel(
             addend[g] = a
 
         def add_terms(g):
-            z = small.tile([P, E, 4], F32, name="pre", tag="pre")
+            z = small.tile([P, E, 4], BF16, name="pre", tag="pre")
             nc.vector.tensor_tensor(
                 out=z[:],
                 in0=hidden[g][:].rearrange("p (j e) -> p e j", j=4),
@@ -272,19 +267,19 @@ def tile_edgenetwork_w_kernel(
         nc.vector.tensor_copy(out=b1_f32[:], in_=b1_rows[:].rearrange("r (p j) -> r j p", j=4))
 
         def quantise_x():
-            for o, tag in enumerate(("acc", "hp")):
+            for o in range(2):
                 words = (x_raw, x_split)[o][:].bitcast(F32)
                 x_out = x_grouped[:, o, :].bitcast(F32).rearrange("w (c e u) -> w c e u", c=4, e=E, u=2)
                 for h in range(2):
-                    copy_out(False, x_out[:, 2 * h : 2 * h + 2], transpose_words(words, 2 * h, o == 1, tag))
+                    copy_out(False, x_out[:, 2 * h : 2 * h + 2], transpose_words(words, 2 * h, o == 1))
                 nc.vector.quantize_mx(
                     out=x_codes[:, o, :].bitcast(FP8X4), scales=x_planes[:, o, :], in_=x_grouped[:, o, :]
                 )
 
         def spread_edge_and_b1():
-            edge_bank = psum.tile([P, 512], F32, name="edge_bank", tag="acc", bufs=2)
+            edge_bank = psum.tile([P, 512], F32, name="edge_bank", tag="tp")
             nc.tensor.matmul(edge_bank[:, 0:E], lhsT=ones[:], rhs=row[:, OUT : OUT + E], start=True, stop=True)
-            b1_bank = psum.tile([P, 512], F32, name="b1_bank", tag="acc", bufs=2)
+            b1_bank = psum.tile([P, 512], F32, name="b1_bank", tag="tp")
             for j in range(4):
                 nc.tensor.transpose(b1_bank[:, j * P : (j + 1) * P], b1_f32[:, j, :], ident[:])
             nc.vector.tensor_copy(out=edge_all[:], in_=edge_bank[:, 0:E])
@@ -295,7 +290,7 @@ def tile_edgenetwork_w_kernel(
 
         def spread_b2():
             for half in range(2):
-                b2_bank = psum.tile([P, 1024], BF16, name="b2_bank", tag="tp", bufs=4)
+                b2_bank = psum.tile([P, 1024], BF16, name="b2_bank", tag="tp")
                 for i in range(2):
                     first = 1024 * half + 512 * i
                     nc.tensor.matmul(
@@ -309,35 +304,21 @@ def tile_edgenetwork_w_kernel(
 
         acc = {}
 
-        def layer2(half, g):
-            if g == 0:
-                tag = ("acc", "tp")[half]
-                for i in range(2):
-                    acc[half, i] = psum.tile([P, 512], F32, name=tag, tag=tag, bufs=(2, 4)[half])
+        def layer2(g, which=pieces):
             a, b = g // 4, g % 4
-            for i in range(2):
-                cols = slice(i * 512, (i + 1) * 512)
-                scale_cols = slice(half * HALF + i * 512, half * HALF + (i + 1) * 512)
+            for lo, hi in which:
+                if g == 0:
+                    acc[lo] = psum.tile([P, 512], F32, name="acc", tag="tp")
                 nc.tensor.matmul_mx(
-                    out=acc[half, i][:],
+                    out=acc[lo][:, 0 : hi - lo],
                     lhsT=h_codes[:, g, :].bitcast(FP8X4),
                     lhsT_scale=h_planes[:, g, :],
-                    rhs=w2_tiles[half, g][:, cols].bitcast(FP8X4),
-                    rhs_scale=w2_planes[4 * b : P, a, scale_cols],
+                    rhs=w2_tiles[g][:, lo:hi].bitcast(FP8X4),
+                    rhs_scale=w2_planes[4 * b : P, a, lo:hi],
                     start=(g == 0),
                     stop=(g == G - 1),
                 )
 
-        def finish(half):
-            for i in range(2):
-                cols = slice(half * HALF + i * 512, half * HALF + (i + 1) * 512)
-                biased = fin.tile([P, 512], F32, name="biased", tag="biased")
-                nc.vector.tensor_tensor(out=biased[:], in0=acc[half, i][:], in1=b2_all[:, cols], op=ADD)
-                result = fin.tile([P, 512], F32, name="result", tag="result")
-                nc.scalar.activation(out=result[:], in_=biased[:], func=ACT.Tanh)
-                nc.sync.dma_start(out=out[:, cols], in_=result[:])
-
-        late_w2 = {8: ((0, 4), (0, 5)), 9: ((0, 6), (0, 7)), 10: ((1, 0), (1, 1)), 11: ((1, 2), (1, 3)), 12: ((1, 4), (1, 5)), 13: ((1, 6),), 14: ((1, 7),)}
         for s in range(1, UNITS + 4):
             if s < UNITS:
                 transposes(s)
@@ -359,27 +340,36 @@ def tile_edgenetwork_w_kernel(
                 quantise_h((s - 5) // 2)
             if s >= 3 and s % 2 == 1 and (s - 3) // 2 < G:
                 make_addend((s - 3) // 2)
+            if s == 4:
+                spread_b2()
+            if s == UNITS:
+                layer2(0)
+            if s == UNITS + 1:
+                layer2(1)
             if 0 <= s - 2 < UNITS:
                 layer1(s - 2)
-            if s >= 7 and s % 2 == 1 and (s - 7) // 2 < 5:
-                layer2(0, (s - 7) // 2)
-            if s == UNITS:
-                spread_b2()
-                layer2(0, 5)
-                layer2(1, 0)
             if s == UNITS + 1:
-                for g in range(1, 4):
-                    layer2(1, g)
+                layer2(2)
+                layer2(3)
             if s == UNITS + 2:
-                layer2(0, 6)
-                layer2(1, 4)
+                layer2(4)
             if s + W1_SLOTS - 1 < UNITS:
                 load_next(s + W1_SLOTS - 1)
-            for half, g in late_w2.get(s, ()):
-                load_w2(half, g)
+            if s == 11:
+                for g in range(G):
+                    load_w2(g)
+                    if g in (0, 2):
+                        for q in range(4):
+                            load_scales(2 * g + q)
 
-        layer2(0, 7)
-        finish(0)
-        for g in range(5, G):
-            layer2(1, g)
-        finish(1)
+        layer2(5)
+        for lo, hi in pieces:
+            layer2(6, ((lo, hi),))
+            layer2(7, ((lo, hi),))
+            biased = fin.tile([P, 512], F32, name="biased", tag="biased", bufs=3)
+            nc.vector.tensor_tensor(
+                out=biased[:, 0 : hi - lo], in0=acc[lo][:, 0 : hi - lo], in1=b2_all[:, lo:hi], op=ADD
+            )
+            result = fin.tile([P, 512], F32, name="result", tag="result", bufs=5)
+            nc.scalar.activation(out=result[:, 0 : hi - lo], in_=biased[:, 0 : hi - lo], func=ACT.Tanh)
+            nc.sync.dma_start(out=out[:, lo:hi], in_=result[:, 0 : hi - lo])

@@ -131,8 +131,7 @@ def tile_edgenetwork_w_kernel(
             load_next(s)
 
         b1_f32 = const.tile([P, 4, P], F32, name="b1_f32")
-        w1_edge = const.tile([P, G, 4], F32, name="w1_edge")
-        b1_col = const.tile([P, G, 4], F32, name="b1_col")
+        b1_col = const.tile([P, G, 4], BF16, name="b1_col")
         edge_all = const.tile([P, E], F32, name="edge_all")
         b2_all = const.tile([P, OUT], BF16, name="b2_all")
         x_split = const.tile([P, D], BF16, name="x_split", align_bytes=64)
@@ -187,10 +186,6 @@ def tile_edgenetwork_w_kernel(
             split_blocks(t[:], raw[s][:, ROW : ROW + D])
             split[s] = t
 
-        def edge_column(s):
-            g, jh = s // 2, s % 2
-            nc.gpsimd.tensor_copy(out=w1_edge[:, g, 2 * jh : 2 * jh + 2], in_=raw[s][:, D : 2 * ROW : ROW])
-
         def copies(s):
             gr = work.tile([P, 4096], BF16, name="grouped", tag="grouped", align_bytes=64)
             grouped[s] = gr
@@ -224,12 +219,13 @@ def tile_edgenetwork_w_kernel(
                     )
 
         def make_addend(g):
-            a = small.tile([P, 4, E], F32, name="addend", tag="addend")
+            a = small.tile([P, 4, E], F32, name="addend", tag="addend", bufs=3)
             for j in range(4):
+                column = j % 2 * ROW + D
                 nc.vector.tensor_scalar(
                     out=a[:, j, :],
                     in0=edge_all[:],
-                    scalar1=w1_edge[:, g, j : j + 1],
+                    scalar1=raw[2 * g + j // 2][:, column : column + 1],
                     scalar2=b1_col[:, g, j : j + 1],
                     op0=MULT,
                     op1=ADD,
@@ -261,7 +257,6 @@ def tile_edgenetwork_w_kernel(
         split_row(0)
         transposes(0)
         copies(0)
-        edge_column(0)
         split_row(1)
         split_blocks(x_split[:], x_raw[:])
         nc.vector.tensor_copy(out=b1_f32[:], in_=b1_rows[:].rearrange("r (p j) -> r j p", j=4))
@@ -326,30 +321,29 @@ def tile_edgenetwork_w_kernel(
             if s >= 4 and s % 2 == 0:
                 add_terms((s - 4) // 2)
                 relu((s - 4) // 2)
-            if s < UNITS:
-                edge_column(s)
             if s + 1 < UNITS:
                 split_row(s + 1)
             if s - 1 < UNITS:
                 quantise(s - 1)
             if s == 1:
                 quantise_x()
-            if s == 2:
+            if s == 1:
                 spread_edge_and_b1()
             if s >= 5 and s % 2 == 1:
                 quantise_h((s - 5) // 2)
-            if s >= 3 and s % 2 == 1 and (s - 3) // 2 < G:
-                make_addend((s - 3) // 2)
+            if s % 2 == 1 and s < UNITS:
+                make_addend(s // 2)
             if s == 4:
                 spread_b2()
             if s == UNITS:
                 layer2(0)
             if s == UNITS + 1:
                 layer2(1)
+                layer2(2, pieces[:1])
             if 0 <= s - 2 < UNITS:
                 layer1(s - 2)
             if s == UNITS + 1:
-                layer2(2)
+                layer2(2, pieces[1:])
                 layer2(3)
             if s == UNITS + 2:
                 layer2(4)

@@ -22,9 +22,10 @@ OUT = 2048
 G = MID // 512
 UNITS = 2 * G
 ROW = D + 1
-W1_SLOTS = 8
-W2_SLOTS = 5
-SPLIT_UNITS = 1
+HALF = OUT // 2
+W1_SLOTS = 4
+W2_SLOTS = 6
+UNIT_END = 4112
 
 FLOPS = 2 * E * (D + 1) * MID + 2 * E * MID * OUT
 
@@ -54,7 +55,7 @@ def tile_edgenetwork_w_kernel(
         fin = ctx.enter_context(tc.tile_pool(name="fin", bufs=4))
         psum = ctx.enter_context(tc.psum_pool(name="psum", bufs=6))
 
-        w1_view = W1.rearrange("(g p h j) k -> g p h (j k)", g=G, p=P, h=2, j=2)
+        w1_view = W1.rearrange("(g p j) k -> g p (j k)", g=G, p=P, j=4)
 
         pieces = ((0, 512), (512, 1024), (1024, 1536), (1536, 1792), (1792, OUT))
 
@@ -70,15 +71,12 @@ def tile_edgenetwork_w_kernel(
         h_grouped = {}
         w2_tiles = {}
 
-        def load_unit(s):
-            r = big.tile([P, 2 * ROW], BF16, name="raw", tag="big", align_bytes=64)
-            g, jh = s // 2, s % 2
-            if s < SPLIT_UNITS:
-                for lo, hi in ((0, 1024), (1024, 2048), (2048, 3072), (3072, 2 * ROW)):
-                    nc.sync.dma_start(out=r[:, lo:hi], in_=w1_view[g][:, jh, lo:hi])
-            else:
-                nc.sync.dma_start(out=r[:], in_=w1_view[g][:, jh, :])
-            raw[s] = r
+        def load_group(g, cuts=()):
+            r = big.tile([P, 4 * ROW], BF16, name="raw", tag="big", align_bytes=64)
+            edges = (0, *cuts, 4 * ROW)
+            for lo, hi in zip(edges, edges[1:]):
+                nc.sync.dma_start(out=r[:, lo:hi], in_=w1_view[g][:, lo:hi])
+            raw[g] = r
 
         def load_scales(i):
             a, q = i // 4, i % 4
@@ -87,15 +85,18 @@ def tile_edgenetwork_w_kernel(
                 in_=W2_scales[4 * a : 4 * a + 4, 4 * q : 4 * q + 4, :].bitcast(I32),
             )
 
-        def load_w2(g):
-            if g < W2_SLOTS:
-                w = w2_pool.tile([P, OUT], U32, name="w2", tag="w2", align_bytes=64)
-            else:
-                w = big.tile([P, OUT], U32, name="w2_late", tag="big", align_bytes=64)
+        def load_w2(g, parts=((0, OUT),)):
+            if g not in w2_tiles:
+                if g < W2_SLOTS:
+                    chunk = w2_pool.tile([P, OUT], U32, name="w2", tag="w2", align_bytes=64)
+                    w2_tiles[g] = chunk[:]
+                else:
+                    last_two = big.tile([P, 2, OUT], U32, name="w2_late", tag="big", align_bytes=64)
+                    for late in range(W2_SLOTS, G):
+                        w2_tiles[late] = last_two[:, late - W2_SLOTS, :]
             src = W2_words[g].rearrange("p n t -> p (n t)").bitcast(I32)
-            for lo, hi in pieces if g == G - 1 else ((0, OUT),):
-                nc.sync.dma_start(out=w[:, lo:hi].bitcast(I32), in_=src[:, lo:hi])
-            w2_tiles[g] = w
+            for lo, hi in parts:
+                nc.sync.dma_start(out=w2_tiles[g][:, lo:hi].bitcast(I32), in_=src[:, lo:hi])
 
         ident = const.tile([P, P], F32, name="ident")
         make_identity(nc, ident[:])
@@ -113,22 +114,18 @@ def tile_edgenetwork_w_kernel(
         w2_planes = const.tile([P, 2, OUT], U8, name="w2_planes", align_bytes=64)
         nc.vector.memset(w2_planes[:].bitcast(I32), 0)
 
-        load_unit(0)
+        load_group(0, (1024, 2048, 3072, UNIT_END))
         nc.scalar.dma_start(out=b1_rows[0:G, :], in_=b1.rearrange("(g c) -> g c", g=G))
         nc.scalar.dma_start(out=row[0:1, OUT : OUT + E], in_=edge_feat.rearrange("(o n) -> o n", o=1))
         nc.scalar.dma_start(out=row[0:1, 0:OUT], in_=b2.rearrange("(o n) -> o n", o=1))
 
-        def load_next(s):
-            load_unit(s)
-
-        load_next(1)
         x_raw = const.tile([P, D], BF16, name="x_raw")
         nc.sync.dma_start(out=x_raw[:, 0:256], in_=dst_node_feat)
         nc.sync.dma_start(out=x_raw[:, 256:1024], in_=dst_node_hidden)
         nc.sync.dma_start(out=x_raw[:, 1024:1280], in_=src_node_feat)
         nc.sync.dma_start(out=x_raw[:, 1280:2048], in_=src_node_hidden)
-        for s in range(2, W1_SLOTS):
-            load_next(s)
+        for g in range(1, W1_SLOTS):
+            load_group(g, (UNIT_END,))
 
         b1_f32 = const.tile([P, 4, P], F32, name="b1_f32")
         b1_col = const.tile([P, G, 4], BF16, name="b1_col")
@@ -166,7 +163,8 @@ def tile_edgenetwork_w_kernel(
                 nc.scalar.copy(out=dst_words, in_=src)
 
         def transposes(s):
-            first_row = raw[s][:, 0:D].bitcast(F32)
+            first = 2 * (s % 2) * ROW
+            first_row = raw[s // 2][:, first : first + D].bitcast(F32)
             second_row = split[s][:].bitcast(F32)
             banks[s] = [
                 transpose_words(first_row, 0, False),
@@ -183,7 +181,8 @@ def tile_edgenetwork_w_kernel(
 
         def split_row(s):
             t = work.tile([P, D], BF16, name="split", tag="split", align_bytes=64)
-            split_blocks(t[:], raw[s][:, ROW : ROW + D])
+            first = (2 * (s % 2) + 1) * ROW
+            split_blocks(t[:], raw[s // 2][:, first : first + D])
             split[s] = t
 
         def copies(s):
@@ -221,11 +220,11 @@ def tile_edgenetwork_w_kernel(
         def make_addend(g):
             a = small.tile([P, 4, E], F32, name="addend", tag="addend", bufs=3)
             for j in range(4):
-                column = j % 2 * ROW + D
+                column = j * ROW + D
                 nc.vector.tensor_scalar(
                     out=a[:, j, :],
                     in0=edge_all[:],
-                    scalar1=raw[2 * g + j // 2][:, column : column + 1],
+                    scalar1=raw[g][:, column : column + 1],
                     scalar2=b1_col[:, g, j : j + 1],
                     op0=MULT,
                     op1=ADD,
@@ -347,14 +346,19 @@ def tile_edgenetwork_w_kernel(
                 layer2(3)
             if s == UNITS + 2:
                 layer2(4)
-            if s + W1_SLOTS - 1 < UNITS:
-                load_next(s + W1_SLOTS - 1)
+            if s % 2 == 1 and W1_SLOTS + s // 2 < G:
+                g = W1_SLOTS + s // 2
+                load_group(g, (UNIT_END,) if g == G - 1 else ())
             if s == 11:
-                for g in range(G):
+                for g in range(W2_SLOTS):
                     load_w2(g)
                     if g in (0, 2):
                         for q in range(4):
                             load_scales(2 * g + q)
+                load_w2(6, ((0, HALF),))
+                load_w2(7, ((0, HALF),))
+                load_w2(6, ((HALF, OUT),))
+                load_w2(7, pieces[2:])
 
         layer2(5)
         for lo, hi in pieces:

from contextlib import ExitStack

import concourse.mybir as mybir
from concourse.masks import make_identity

F32 = mybir.dt.float32
BF16 = mybir.dt.bfloat16
I32 = mybir.dt.int32
U32 = mybir.dt.uint32
U8 = mybir.dt.uint8
FP8X4 = mybir.dt.float8_e4m3fn_x4
ADD = mybir.AluOpType.add
MULT = mybir.AluOpType.mult
MAX = mybir.AluOpType.max
ACT = mybir.ActivationFunctionType

P = 128
E = 128
D = 2048
MID = 4096
OUT = 2048
G = MID // 512
UNITS = 2 * G
ROW = D + 1
HALF = OUT // 2
W1_SLOTS = 4
W2_SLOTS = 6
UNIT_END = 4112

FLOPS = 2 * E * (D + 1) * MID + 2 * E * MID * OUT


def tile_edgenetwork_w_kernel(
    tc,
    dst_node_feat,
    dst_node_hidden,
    src_node_feat,
    src_node_hidden,
    edge_feat,
    W1,
    b1,
    W2_words,
    W2_scales,
    b2,
    out,
):
    nc = tc.nc
    with ExitStack() as ctx:
        ctx.enter_context(tc.manual_schedule())
        const = ctx.enter_context(tc.tile_pool(name="const", bufs=1))
        big = ctx.enter_context(tc.tile_pool(name="big", bufs=W1_SLOTS))
        w2_pool = ctx.enter_context(tc.tile_pool(name="w2_pool", bufs=W2_SLOTS))
        work = ctx.enter_context(tc.tile_pool(name="work", bufs=3))
        small = ctx.enter_context(tc.tile_pool(name="small", bufs=2))
        fin = ctx.enter_context(tc.tile_pool(name="fin", bufs=4))
        psum = ctx.enter_context(tc.psum_pool(name="psum", bufs=6))

        w1_view = W1.rearrange("(g p j) k -> g p (j k)", g=G, p=P, j=4)

        pieces = ((0, 512), (512, 1024), (1024, 1536), (1536, 1792), (1792, OUT))

        raw = {}
        split = {}
        banks = {}
        grouped = {}
        codes = {}
        planes1 = {}
        hidden = {}
        addend = {}
        pre = {}
        h_grouped = {}
        w2_tiles = {}

        def load_group(g, cuts=()):
            r = big.tile([P, 4 * ROW], BF16, name="raw", tag="big", align_bytes=64)
            edges = (0, *cuts, 4 * ROW)
            for lo, hi in zip(edges, edges[1:]):
                nc.sync.dma_start(out=r[:, lo:hi], in_=w1_view[g][:, lo:hi])
            raw[g] = r

        def load_scales(i):
            a, q = i // 4, i % 4
            nc.sync.dma_start(
                out=w2_planes[32 * q : 32 * q + 16, a, :].bitcast(I32),
                in_=W2_scales[4 * a : 4 * a + 4, 4 * q : 4 * q + 4, :].bitcast(I32),
            )

        def load_w2(g, parts=((0, OUT),)):
            if g not in w2_tiles:
                if g < W2_SLOTS:
                    chunk = w2_pool.tile([P, OUT], U32, name="w2", tag="w2", align_bytes=64)
                    w2_tiles[g] = chunk[:]
                else:
                    last_two = big.tile([P, 2, OUT], U32, name="w2_late", tag="big", align_bytes=64)
                    for late in range(W2_SLOTS, G):
                        w2_tiles[late] = last_two[:, late - W2_SLOTS, :]
            src = W2_words[g].rearrange("p n t -> p (n t)").bitcast(I32)
            for lo, hi in parts:
                nc.sync.dma_start(out=w2_tiles[g][:, lo:hi].bitcast(I32), in_=src[:, lo:hi])

        ident = const.tile([P, P], F32, name="ident")
        make_identity(nc, ident[:])
        warm_in = const.tile([P, 1], F32, name="warm_in")
        warm_out = const.tile([P, 1], F32, name="warm_out")
        nc.vector.memset(warm_in[:], 0.0)
        nc.scalar.activation(out=warm_out[:], in_=warm_in[:], func=ACT.Tanh)

        b1_rows = const.tile([P, 512], BF16, name="b1_rows")
        nc.vector.memset(b1_rows[:].bitcast(I32), 0)
        row = const.tile([P, OUT + E], BF16, name="row")
        nc.vector.memset(row[:].bitcast(I32), 0)
        ones = const.tile([P, P], BF16, name="ones")
        nc.vector.memset(ones[:], 1.0)
        w2_planes = const.tile([P, 2, OUT], U8, name="w2_planes", align_bytes=64)
        nc.vector.memset(w2_planes[:].bitcast(I32), 0)

        load_group(0, (1024, 2048, 3072, UNIT_END))
        nc.scalar.dma_start(out=b1_rows[0:G, :], in_=b1.rearrange("(g c) -> g c", g=G))
        nc.scalar.dma_start(out=row[0:1, OUT : OUT + E], in_=edge_feat.rearrange("(o n) -> o n", o=1))
        nc.scalar.dma_start(out=row[0:1, 0:OUT], in_=b2.rearrange("(o n) -> o n", o=1))

        x_raw = const.tile([P, D], BF16, name="x_raw")
        nc.sync.dma_start(out=x_raw[:, 0:256], in_=dst_node_feat)
        nc.sync.dma_start(out=x_raw[:, 256:1024], in_=dst_node_hidden)
        nc.sync.dma_start(out=x_raw[:, 1024:1280], in_=src_node_feat)
        nc.sync.dma_start(out=x_raw[:, 1280:2048], in_=src_node_hidden)
        for g in range(1, W1_SLOTS):
            load_group(g, (UNIT_END,))

        b1_f32 = const.tile([P, 4, P], F32, name="b1_f32")
        b1_col = const.tile([P, G, 4], BF16, name="b1_col")
        edge_all = const.tile([P, E], F32, name="edge_all")
        b2_all = const.tile([P, OUT], BF16, name="b2_all")
        x_split = const.tile([P, D], BF16, name="x_split", align_bytes=64)
        x_grouped = const.tile([P, 2, D], BF16, name="x_grouped", align_bytes=64)
        x_codes = const.tile([P, 2, D // 4], U32, name="x_codes", align_bytes=64)
        x_planes = const.tile([P, 2, D // 4], U8, name="x_planes", align_bytes=64)
        h_codes = const.tile([P, G, E], U32, name="h_codes", align_bytes=64)
        h_planes = const.tile([P, G, E], U8, name="h_planes", align_bytes=64)

        def transpose_words(src_words, first_pass, is_split):
            bank = psum.tile([P, 512], F32, name="tp", tag="tp")
            for cc in range(2):
                for u in range(2):
                    if is_split:
                        first = 512 * u + P * (first_pass + cc)
                        words = src_words[:, first : first + P]
                    else:
                        first = 256 * (first_pass + cc)
                        words = src_words[:, first + u : first + 256 : 2]
                    nc.tensor.transpose(
                        bank[:, (2 * cc + u) * P : (2 * cc + u + 1) * P],
                        words,
                        ident[:],
                    )
            return bank

        def copy_out(engine_is_vector, dst_words, bank):
            src = bank[:].rearrange("w (c u p) -> w c p u", c=2, u=2, p=P)
            if engine_is_vector:
                nc.vector.tensor_copy(out=dst_words, in_=src)
            else:
                nc.scalar.copy(out=dst_words, in_=src)

        def transposes(s):
            first = 2 * (s % 2) * ROW
            first_row = raw[s // 2][:, first : first + D].bitcast(F32)
            second_row = split[s][:].bitcast(F32)
            banks[s] = [
                transpose_words(first_row, 0, False),
                transpose_words(first_row, 2, False),
                transpose_words(second_row, 0, True),
                transpose_words(second_row, 2, True),
            ]

        def split_blocks(dst, src):
            nc.vector.tensor_copy(
                out=dst.rearrange("p (u b e) -> p u b e", u=2, e=16),
                in_=src.rearrange("p (b u e) -> p u b e", u=2, e=16),
            )

        def split_row(s):
            t = work.tile([P, D], BF16, name="split", tag="split", align_bytes=64)
            first = (2 * (s % 2) + 1) * ROW
            split_blocks(t[:], raw[s // 2][:, first : first + D])
            split[s] = t

        def copies(s):
            gr = work.tile([P, 4096], BF16, name="grouped", tag="grouped", align_bytes=64)
            grouped[s] = gr
            words = gr[:].bitcast(F32).rearrange("w (o p u) -> w o p u", o=8, p=P, u=2)
            for b in range(4):
                copy_out(False, words[:, 2 * b : 2 * b + 2], banks[s][b])

        def quantise(s):
            c = work.tile([P, 1024], U32, name="codes", tag="codes", align_bytes=64)
            pl = work.tile([P, 1024], U8, name="planes", tag="planes", align_bytes=64)
            nc.vector.quantize_mx(out=c[:].bitcast(FP8X4), scales=pl[:], in_=grouped[s][:])
            codes[s] = c
            planes1[s] = pl

        def layer1(s):
            g, jh = s // 2, s % 2
            if jh == 0:
                hidden[g] = psum.tile([P, 512], F32, name="hp", tag="hp", bufs=2)
            for jj in range(2):
                j = 2 * jh + jj
                for c in range(4):
                    o = 4 * jj + c
                    nc.tensor.matmul_mx(
                        out=hidden[g][:, j * E : (j + 1) * E],
                        lhsT=codes[s][:, o * P : (o + 1) * P].bitcast(FP8X4),
                        lhsT_scale=planes1[s][:, o * P : (o + 1) * P],
                        rhs=x_codes[:, jj, c * E : (c + 1) * E].bitcast(FP8X4),
                        rhs_scale=x_planes[:, jj, c * E : (c + 1) * E],
                        start=(c == 0),
                        stop=(c == 3),
                    )

        def make_addend(g):
            a = small.tile([P, 4, E], F32, name="addend", tag="addend", bufs=3)
            for j in range(4):
                column = j * ROW + D
                nc.vector.tensor_scalar(
                    out=a[:, j, :],
                    in0=edge_all[:],
                    scalar1=raw[g][:, column : column + 1],
                    scalar2=b1_col[:, g, j : j + 1],
                    op0=MULT,
                    op1=ADD,
                )
            addend[g] = a

        def add_terms(g):
            z = small.tile([P, E, 4], BF16, name="pre", tag="pre")
            nc.vector.tensor_tensor(
                out=z[:],
                in0=hidden[g][:].rearrange("p (j e) -> p e j", j=4),
                in1=addend[g][:].rearrange("p j e -> p e j"),
                op=ADD,
            )
            pre[g] = z

        def relu(g):
            hg = small.tile([P, 4 * E], BF16, name="h_grouped", tag="h_grouped", align_bytes=64)
            nc.vector.tensor_scalar(
                out=hg[:], in0=pre[g][:].rearrange("p e j -> p (e j)"), scalar1=0.0, scalar2=None, op0=MAX
            )
            h_grouped[g] = hg

        def quantise_h(g):
            nc.vector.quantize_mx(
                out=h_codes[:, g, :].bitcast(FP8X4), scales=h_planes[:, g, :], in_=h_grouped[g][:]
            )

        split_row(0)
        transposes(0)
        copies(0)
        split_row(1)
        split_blocks(x_split[:], x_raw[:])
        nc.vector.tensor_copy(out=b1_f32[:], in_=b1_rows[:].rearrange("r (p j) -> r j p", j=4))

        def quantise_x():
            for o in range(2):
                words = (x_raw, x_split)[o][:].bitcast(F32)
                x_out = x_grouped[:, o, :].bitcast(F32).rearrange("w (c e u) -> w c e u", c=4, e=E, u=2)
                for h in range(2):
                    copy_out(False, x_out[:, 2 * h : 2 * h + 2], transpose_words(words, 2 * h, o == 1))
                nc.vector.quantize_mx(
                    out=x_codes[:, o, :].bitcast(FP8X4), scales=x_planes[:, o, :], in_=x_grouped[:, o, :]
                )

        def spread_edge_and_b1():
            edge_bank = psum.tile([P, 512], F32, name="edge_bank", tag="tp")
            nc.tensor.matmul(edge_bank[:, 0:E], lhsT=ones[:], rhs=row[:, OUT : OUT + E], start=True, stop=True)
            b1_bank = psum.tile([P, 512], F32, name="b1_bank", tag="tp")
            for j in range(4):
                nc.tensor.transpose(b1_bank[:, j * P : (j + 1) * P], b1_f32[:, j, :], ident[:])
            nc.vector.tensor_copy(out=edge_all[:], in_=edge_bank[:, 0:E])
            nc.vector.tensor_copy(
                out=b1_col[:].rearrange("p g j -> p j g"),
                in_=b1_bank[:].rearrange("p (j r) -> p j r", j=4)[:, :, 0:G],
            )

        def spread_b2():
            for half in range(2):
                b2_bank = psum.tile([P, 1024], BF16, name="b2_bank", tag="tp")
                for i in range(2):
                    first = 1024 * half + 512 * i
                    nc.tensor.matmul(
                        b2_bank[:, 512 * i : 512 * (i + 1)],
                        lhsT=ones[:],
                        rhs=row[:, first : first + 512],
                        start=True,
                        stop=True,
                    )
                nc.scalar.copy(out=b2_all[:, 1024 * half : 1024 * (half + 1)], in_=b2_bank[:])

        acc = {}

        def layer2(g, which=pieces):
            a, b = g // 4, g % 4
            for lo, hi in which:
                if g == 0:
                    acc[lo] = psum.tile([P, 512], F32, name="acc", tag="tp")
                nc.tensor.matmul_mx(
                    out=acc[lo][:, 0 : hi - lo],
                    lhsT=h_codes[:, g, :].bitcast(FP8X4),
                    lhsT_scale=h_planes[:, g, :],
                    rhs=w2_tiles[g][:, lo:hi].bitcast(FP8X4),
                    rhs_scale=w2_planes[4 * b : P, a, lo:hi],
                    start=(g == 0),
                    stop=(g == G - 1),
                )

        for s in range(1, UNITS + 4):
            if s < UNITS:
                transposes(s)
                copies(s)
            if s >= 4 and s % 2 == 0:
                add_terms((s - 4) // 2)
                relu((s - 4) // 2)
            if s + 1 < UNITS:
                split_row(s + 1)
            if s - 1 < UNITS:
                quantise(s - 1)
            if s == 1:
                quantise_x()
            if s == 1:
                spread_edge_and_b1()
            if s >= 5 and s % 2 == 1:
                quantise_h((s - 5) // 2)
            if s % 2 == 1 and s < UNITS:
                make_addend(s // 2)
            if s == 4:
                spread_b2()
            if s == UNITS:
                layer2(0)
            if s == UNITS + 1:
                layer2(1)
                layer2(2, pieces[:1])
            if 0 <= s - 2 < UNITS:
                layer1(s - 2)
            if s == UNITS + 1:
                layer2(2, pieces[1:])
                layer2(3)
            if s == UNITS + 2:
                layer2(4)
            if s % 2 == 1 and W1_SLOTS + s // 2 < G:
                g = W1_SLOTS + s // 2
                load_group(g, (UNIT_END,) if g == G - 1 else ())
            if s == 11:
                for g in range(W2_SLOTS):
                    load_w2(g)
                    if g in (0, 2):
                        for q in range(4):
                            load_scales(2 * g + q)
                load_w2(6, ((0, HALF),))
                load_w2(7, ((0, HALF),))
                load_w2(6, ((HALF, OUT),))
                load_w2(7, pieces[2:])

        layer2(5)
        for lo, hi in pieces:
            layer2(6, ((lo, hi),))
            layer2(7, ((lo, hi),))
            biased = fin.tile([P, 512], F32, name="biased", tag="biased", bufs=3)
            nc.vector.tensor_tensor(
                out=biased[:, 0 : hi - lo], in0=acc[lo][:, 0 : hi - lo], in1=b2_all[:, lo:hi], op=ADD
            )
            result = fin.tile([P, 512], F32, name="result", tag="result", bufs=5)
            nc.scalar.activation(out=result[:, 0 : hi - lo], in_=biased[:, 0 : hi - lo], func=ACT.Tanh)
            nc.sync.dma_start(out=out[:, lo:hi], in_=result[:, 0 : hi - lo])
